import numpy as np
import ml_dtypes


def mxq(x, axis, fmt="e4m3"):
    dtype, down = {"e4m3": (ml_dtypes.float8_e4m3fn, 7), "e5m2": (ml_dtypes.float8_e5m2, 14)}[fmt]
    v = np.moveaxis(np.asarray(x, np.float32).astype(ml_dtypes.bfloat16).astype(np.float64), axis, -1)
    blocks = v.reshape(v.shape[:-1] + (-1, 32))
    amax = np.abs(blocks).max(-1, keepdims=True)
    byte = np.maximum(np.where(amax > 0, np.frexp(amax)[1] - 1 + 127, 0) - down, 1)
    scale = np.exp2(byte - 127.0)
    codes = (blocks / scale).astype(np.float32).astype(dtype).astype(np.float64)
    return np.moveaxis((codes * scale).reshape(v.shape), -1, axis)


WIDE = False


def mx_kscale(k):
    if not WIDE:
        return np.ones(k)
    levels = np.array([10, -10, 5, -5, 0])
    if k % 512:
        return np.exp2(np.random.permutation(np.resize(levels, k // 32))).repeat(32)
    a = np.empty((k // 512, 16))
    for p in range(k // 512):
        a[p, :8] = np.random.permutation(np.resize(levels, 8))
        for g in range(8):
            far = levels[np.abs(levels - a[p, g]) >= 10]
            a[p, g + 8] = far[np.random.randint(len(far))]
    return np.exp2(a.ravel()).repeat(32)


BF16 = ml_dtypes.bfloat16


def bf(x):
    return np.asarray(x, np.float32).astype(BF16)


def f64(x):
    return np.asarray(x).astype(np.float64)


C, G, P, E = 8192, 1024, 8, 64


def setup_inputs():
    s = mx_kscale(G)
    return {"x": bf(np.random.standard_normal((C, G)) * s),
            "mask": bf(np.random.randint(0, 2, (G, P))),
            "W": bf(np.random.standard_normal((G, P * E)) * 1.4 / np.sqrt(G) / s[:, None]),
            "b": bf(np.random.standard_normal(P * E) * 0.3)}


def reference(x, mask, W, b):
    mask_rep = np.repeat(f64(mask), E, axis=1)
    out = (mxq(f64(x), 1, "e4m3") @ mxq(f64(W) * mask_rep, 0, "e4m3")) + f64(b)
    out = out.reshape(C, E, P).transpose(0, 2, 1)
    return out

@@ -1,0 +1,236 @@
+from contextlib import ExitStack
+
+import concourse.mybir as mybir
+from concourse.masks import make_identity
+
+F32 = mybir.dt.float32
+BF16 = mybir.dt.bfloat16
+U32 = mybir.dt.uint32
+U8 = mybir.dt.uint8
+FP8X4 = mybir.dt.float8_e4m3fn_x4
+ADD = mybir.AluOpType.add
+MULT = mybir.AluOpType.mult
+
+C, G, NP, E = 8192, 1024, 8, 64
+J = NP * E
+P = 128
+NT = C // P
+FLOPS = 2 * C * G * J
+
+RUNS = [4,4,4,4,4,4,4,4,4,4,4,4,4,4,4,2,2]
+LOADS = [4,4,4,4,8,8,8,8,8,8]
+STORES = [4,4,4,4,4,4,4,4,4,4,4,4,4,4,4,2,2]
+XBUFS = {4:4,8:3}
+OBUFS = {2:2,4:6}
+LEAD = 24
+QW = 2
+GBQ = 6
+CBQ = 6
+LA = 1
+assert sum(RUNS) == NT and sum(LOADS) == NT and sum(STORES) == NT
+
+
+def tile_featureembed_t_kernel(tc, x, mask, W, b, out):
+    nc = tc.nc
+    x_view = x.rearrange("(p t) k -> p t k", t=NT)
+    out_view = out.rearrange("(p t) a e -> p t (a e)", t=NT)
+
+    with ExitStack() as ctx:
+        const = ctx.enter_context(tc.tile_pool(name="const", bufs=1))
+        xpool = ctx.enter_context(tc.tile_pool(name="xpool", bufs=1))
+        gpool = ctx.enter_context(tc.tile_pool(name="gpool", bufs=GBQ))
+        cpool = ctx.enter_context(tc.tile_pool(name="cpool", bufs=CBQ))
+        opool = ctx.enter_context(tc.tile_pool(name="opool", bufs=1))
+        psum = ctx.enter_context(tc.psum_pool(name="psum", bufs=1))
+        ctx.enter_context(tc.manual_schedule())
+
+        brow = const.tile([P, J], BF16, name="brow")
+        ones = const.tile([P, P], BF16, name="ones")
+        ident = const.tile([P, P], F32, name="ident")
+        nc.gpsimd.memset(brow[:], 0.0)
+        nc.gpsimd.memset(ones[:], 1.0)
+        make_identity(nc, ident[:])
+
+        mk = const.tile([P, 64], BF16, name="mk")
+        nc.scalar.dma_start(
+            out=mk[:].rearrange("q (g r) -> q g r", g=2),
+            in_=mask.rearrange("(g q t) m -> q g (t m)", g=2, q=P, t=4),
+        )
+        nc.scalar.dma_start(out=brow[0:1, :], in_=b.unsqueeze(0))
+
+        w_raw = const.tile([P, 4096], BF16, name="w_raw")
+        for g in range(2):
+            nc.sync.dma_start(
+                out=w_raw[:, g * 2048 : (g + 1) * 2048],
+                in_=W[g * 512 : (g + 1) * 512, :].rearrange("(q t) j -> q (t j)", t=4),
+            )
+
+        x_of = {}
+        load_first = []
+        t0 = 0
+        for n in LOADS:
+            load_first.append(t0)
+            t0 += n
+        state = {"next_load": 0}
+
+        def issue_loads(limit):
+            while state["next_load"] < len(LOADS):
+                li = state["next_load"]
+                n = LOADS[li]
+                first = load_first[li]
+                if first + n > limit:
+                    break
+                x_sb = xpool.tile([P, n, G], BF16, name="x%d" % n, tag="x%d" % n, bufs=XBUFS[n])
+                nc.sync.dma_start(out=x_sb[:], in_=x_view[:, first : first + n, :])
+                x_f = x_sb[:].bitcast(F32)
+                for k in range(n):
+                    x_of[first + k] = (x_f, k)
+                state["next_load"] = li + 1
+
+        issue_loads(LEAD)
+
+        mk_exp = const.tile([P, 512], BF16, name="mk_exp")
+        nc.vector.tensor_copy(
+            out=mk_exp[:].rearrange("q (r i) -> q r i", i=8),
+            in_=mk[:].unsqueeze(2).to_broadcast([P, 64, 8]),
+        )
+        w_grp = const.tile([P, 4096], BF16, name="w_grp", align_bytes=64)
+        w_codes = const.tile([P, 1024], U32, name="w_codes", align_bytes=64)
+        w_scales = const.tile([P, 1024], U8, name="w_scales", align_bytes=64)
+        for g in range(2):
+            for h in range(2):
+                nc.vector.tensor_tensor(
+                    out=w_grp[:, g * 2048 + h * 1024 : g * 2048 + (h + 1) * 1024].rearrange(
+                        "q (a e t) -> q e t a", a=4, t=4
+                    ),
+                    in0=w_raw[:, g * 2048 : (g + 1) * 2048].rearrange("q (t e a) -> q e t a", t=4, a=NP)[
+                        :, :, :, h * 4 : (h + 1) * 4
+                    ],
+                    in1=mk_exp[:, g * 256 : (g + 1) * 256]
+                    .rearrange("q (t e) -> q e t", t=4)
+                    .unsqueeze(3)
+                    .to_broadcast([P, E, 4, 4]),
+                    op=MULT,
+                )
+        for g in range(2):
+            nc.vector.quantize_mx(
+                out=w_codes[:, g * 512 : (g + 1) * 512].bitcast(FP8X4),
+                scales=w_scales[:, g * 512 : (g + 1) * 512],
+                in_=w_grp[:, g * 2048 : (g + 1) * 2048],
+            )
+
+        bias = const.tile([P, J], F32, name="bias")
+
+        def make_bias():
+            yb = psum.tile([P, J], F32, name="yb", tag="y0")
+            nc.tensor.matmul(out=yb[:], lhsT=ones[:], rhs=brow[:], start=True, stop=True)
+            nc.scalar.copy(
+                out=bias[:].rearrange("q (a e) -> q a e", a=NP),
+                in_=yb[:].rearrange("q (e a) -> q a e", a=NP),
+            )
+
+        run_first = []
+        t0 = 0
+        for n in RUNS:
+            run_first.append(t0)
+            t0 += n
+        chunks = []
+        chunk_of = {}
+        run_chunks = []
+        for r in range(len(RUNS)):
+            mine = []
+            for o in range(0, RUNS[r], QW):
+                w = min(QW, RUNS[r] - o)
+                mine.append(len(chunks))
+                for k in range(w):
+                    chunk_of[run_first[r] + o + k] = (len(chunks), k)
+                chunks.append((run_first[r] + o, w))
+            run_chunks.append(mine)
+        store_of = {}
+        t0 = 0
+        for si in range(len(STORES)):
+            for k in range(STORES[si]):
+                store_of[t0 + k] = (si, k, t0)
+            t0 += STORES[si]
+
+        grp_of = {}
+        code_of = {}
+        o_of = {}
+        y_of = {}
+
+        def transpose_tile(t):
+            q, k = chunk_of[t]
+            w = chunks[q][1]
+            if k == 0:
+                grp_of[q] = gpool.tile([P, QW * 1024], BF16, name="grp", tag="grp", align_bytes=64)
+            grp_f = grp_of[q][:].bitcast(F32)
+            x_f, i = x_of[t]
+            xt = psum.tile([P, 4, P], F32, name="xt%d" % (t % 4), tag="xt%d" % (t % 4))
+            for a in range(4):
+                first = (a // 2) * 256 + a % 2
+                nc.tensor.transpose(xt[:, a, :], x_f[:, i, first : (a // 2 + 1) * 256 : 2], ident[:])
+            nc.scalar.copy(
+                out=grp_f[:, k * 512 : (k + 1) * 512].rearrange("q (g c u) -> q g c u", g=2, u=2),
+                in_=xt[:].rearrange("q (g u) c -> q g c u", u=2),
+            )
+
+        def quantise(q):
+            w = chunks[q][1]
+            codes = cpool.tile([P, QW * 256], U32, name="codes", tag="codes", align_bytes=64)
+            scales = cpool.tile([P, QW * 256], U8, name="scales", tag="scales", align_bytes=64)
+            code_of[q] = (codes, scales)
+            nc.vector.quantize_mx(
+                out=codes[:, 0 : w * 256].bitcast(FP8X4),
+                scales=scales[:, 0 : w * 256],
+                in_=grp_of[q][:, 0 : w * 1024],
+            )
+
+        def multiply(t):
+            q, k = chunk_of[t]
+            codes, scales = code_of[q]
+            y = psum.tile([P, J], F32, name="y%d" % (t % 4), tag="y%d" % (t % 4))
+            for g in range(2):
+                cols = slice((k * 2 + g) * P, (k * 2 + g + 1) * P)
+                nc.tensor.matmul_mx(
+                    out=y[:],
+                    lhsT=codes[:, cols].bitcast(FP8X4),
+                    lhsT_scale=scales[:, cols],
+                    rhs=w_codes[:, g * 512 : (g + 1) * 512].bitcast(FP8X4),
+                    rhs_scale=w_scales[:, g * 512 : (g + 1) * 512],
+                    start=(g == 0),
+                    stop=(g == 1),
+                )
+            y_of[t] = y
+
+        def add_bias(t):
+            si, k, first = store_of[t]
+            n = STORES[si]
+            if k == 0:
+                o_of[si] = opool.tile([P, n, J], F32, name="o%d" % n, tag="o%d" % n, bufs=OBUFS[n])
+            o_sb = o_of[si]
+            nc.vector.tensor_tensor(out=o_sb[:, k, :], in0=y_of[t][:], in1=bias[:], op=ADD)
+            if k == n - 1:
+                nc.sync.dma_start(out=out_view[:, first : first + n, :], in_=o_sb[:])
+
+        NR = len(RUNS)
+        for s in range(NR + LA):
+            if s < NR:
+                for t in range(run_first[s], run_first[s] + RUNS[s]):
+                    transpose_tile(t)
+                issue_loads(run_first[s] + RUNS[s] + LEAD)
+            if s == 0:
+                make_bias()
+            m = s - LA
+            qs = run_chunks[s] if s < NR else []
+            ts = list(range(run_first[m], run_first[m] + RUNS[m])) if m >= 0 else []
+            per = (len(ts) + len(qs) - 1) // len(qs) if qs else len(ts)
+            done = 0
+            for q in qs:
+                quantise(q)
+                for t in ts[done : done + per]:
+                    multiply(t)
+                    add_bias(t)
+                done += per
+            for t in ts[done:]:
+                multiply(t)
+                add_bias(t)

@@ -40,6 +40,7 @@ def tile_featureembed_t_kernel(tc, x, mask, W, b, out):
         xpool = ctx.enter_context(tc.tile_pool(name="xpool", bufs=1))
         gpool = ctx.enter_context(tc.tile_pool(name="gpool", bufs=GBQ))
         cpool = ctx.enter_context(tc.tile_pool(name="cpool", bufs=CBQ))
+        xppool = ctx.enter_context(tc.tile_pool(name="xppool", bufs=12))
         opool = ctx.enter_context(tc.tile_pool(name="opool", bufs=1))
         psum = ctx.enter_context(tc.psum_pool(name="psum", bufs=1))
         ctx.enter_context(tc.manual_schedule())
@@ -158,17 +159,29 @@ def tile_featureembed_t_kernel(tc, x, mask, W, b, out):
         o_of = {}
         y_of = {}
 
+        xp_of = {}
+
+        def permute_tile(t):
+            x_f, i = x_of[t]
+            xp = xppool.tile([P, 512], F32, name="xp", tag="xp")
+            xp_of[t] = xp
+            dst = xp[:].rearrange("p (g u q) -> p g u q", g=2, u=2)
+            src = x_f[:, i, :].rearrange("p (g q u) -> p g u q", g=2, u=2)
+            if t % 4 == 3:
+                nc.vector.tensor_copy(out=dst, in_=src)
+            else:
+                nc.scalar.copy(out=dst, in_=src)
+
         def transpose_tile(t):
             q, k = chunk_of[t]
             w = chunks[q][1]
             if k == 0:
                 grp_of[q] = gpool.tile([P, QW * 1024], BF16, name="grp", tag="grp", align_bytes=64)
             grp_f = grp_of[q][:].bitcast(F32)
-            x_f, i = x_of[t]
+            xp = xp_of[t]
             xt = psum.tile([P, 4, P], F32, name="xt%d" % (t % 4), tag="xt%d" % (t % 4))
             for a in range(4):
-                first = (a // 2) * 256 + a % 2
-                nc.tensor.transpose(xt[:, a, :], x_f[:, i, first : (a // 2 + 1) * 256 : 2], ident[:])
+                nc.tensor.transpose(xt[:, a, :], xp[:, a * P : (a + 1) * P], ident[:])
             nc.scalar.copy(
                 out=grp_f[:, k * 512 : (k + 1) * 512].rearrange("q (g c u) -> q g c u", g=2, u=2),
                 in_=xt[:].rearrange("q (g u) c -> q g c u", u=2),
@@ -213,11 +226,16 @@ def tile_featureembed_t_kernel(tc, x, mask, W, b, out):
                 nc.sync.dma_start(out=out_view[:, first : first + n, :], in_=o_sb[:])
 
         NR = len(RUNS)
+        for t in range(RUNS[0]):
+            permute_tile(t)
         for s in range(NR + LA):
             if s < NR:
                 for t in range(run_first[s], run_first[s] + RUNS[s]):
                     transpose_tile(t)
                 issue_loads(run_first[s] + RUNS[s] + LEAD)
+            if s + 1 < NR:
+                for t in range(run_first[s + 1], run_first[s + 1] + RUNS[s + 1]):
+                    permute_tile(t)
             if s == 0:
                 make_bias()
             m = s - LA

@@ -167,7 +167,7 @@ def tile_featureembed_t_kernel(tc, x, mask, W, b, out):
             xp_of[t] = xp
             dst = xp[:].rearrange("p (g u q) -> p g u q", g=2, u=2)
             src = x_f[:, i, :].rearrange("p (g q u) -> p g u q", g=2, u=2)
-            if t % 4 == 3:
+            if t % 8 in (1, 3, 6):
                 nc.vector.tensor_copy(out=dst, in_=src)
             else:
                 nc.scalar.copy(out=dst, in_=src)

@@ -17,17 +17,21 @@ P = 128
 NT = C // P
 FLOPS = 2 * C * G * J
 
-RUNS = [4,4,4,4,4,4,4,4,4,4,4,4,4,4,4,2,2]
-LOADS = [4,4,4,4,8,8,8,8,8,8]
-STORES = [4,4,4,4,4,4,4,4,4,4,4,4,4,4,4,2,2]
-XBUFS = {4:4,8:3}
-OBUFS = {2:2,4:6}
-LEAD = 24
+CH = 4
+RUNS = [2, 2] + [4] * 14 + [2, 2]
+LOADS = [2, 2] + [4] * 15
+STORES = [4] * 15 + [2, 2]
 QW = 2
 GBQ = 6
 CBQ = 6
+XPB = 12
 LA = 1
+PL = 1
 assert sum(RUNS) == NT and sum(LOADS) == NT and sum(STORES) == NT
+
+
+def vector_permutes(t):
+    return t >= 8 and t % 8 in (1, 3, 6)
 
 
 def tile_featureembed_t_kernel(tc, x, mask, W, b, out):
@@ -37,11 +41,10 @@ def tile_featureembed_t_kernel(tc, x, mask, W, b, out):
 
     with ExitStack() as ctx:
         const = ctx.enter_context(tc.tile_pool(name="const", bufs=1))
-        xpool = ctx.enter_context(tc.tile_pool(name="xpool", bufs=1))
+        slots = ctx.enter_context(tc.tile_pool(name="slots", bufs=1))
+        xppool = ctx.enter_context(tc.tile_pool(name="xppool", bufs=XPB))
         gpool = ctx.enter_context(tc.tile_pool(name="gpool", bufs=GBQ))
         cpool = ctx.enter_context(tc.tile_pool(name="cpool", bufs=CBQ))
-        xppool = ctx.enter_context(tc.tile_pool(name="xppool", bufs=12))
-        opool = ctx.enter_context(tc.tile_pool(name="opool", bufs=1))
         psum = ctx.enter_context(tc.psum_pool(name="psum", bufs=1))
         ctx.enter_context(tc.manual_schedule())
 
@@ -53,49 +56,54 @@ def tile_featureembed_t_kernel(tc, x, mask, W, b, out):
         make_identity(nc, ident[:])
 
         mk = const.tile([P, 64], BF16, name="mk")
-        nc.scalar.dma_start(
+        nc.sync.dma_start(
             out=mk[:].rearrange("q (g r) -> q g r", g=2),
             in_=mask.rearrange("(g q t) m -> q g (t m)", g=2, q=P, t=4),
         )
-        nc.scalar.dma_start(out=brow[0:1, :], in_=b.unsqueeze(0))
+        w_raw = slots.tile([P, 4096], BF16, name="w_raw", tag="s16", align_bytes=64)
+        w_grp = slots.tile([P, 4096], BF16, name="w_grp", tag="s17", align_bytes=64)
 
-        w_raw = const.tile([P, 4096], BF16, name="w_raw")
-        for g in range(2):
+        def load_w(g):
             nc.sync.dma_start(
                 out=w_raw[:, g * 2048 : (g + 1) * 2048],
                 in_=W[g * 512 : (g + 1) * 512, :].rearrange("(q t) j -> q (t j)", t=4),
             )
 
         x_of = {}
-        load_first = []
-        t0 = 0
-        for n in LOADS:
-            load_first.append(t0)
+        x_slots = {}
+
+        def load_x(first, n):
+            ci = first // CH
+            if ci not in x_slots:
+                x_slots[ci] = slots.tile([P, CH, G], BF16, name="x%d" % ci, tag="s%d" % ci, align_bytes=64)
+            x_sb = x_slots[ci]
+            o = first % CH
+            nc.sync.dma_start(out=x_sb[:, o : o + n, :], in_=x_view[:, first : first + n, :])
+            for k in range(n):
+                x_of[first + k] = (x_sb[:].bitcast(F32), o + k)
+
+        load_w(0)
+        load_x(0, 2)
+        nc.sync.dma_start(out=brow[0:1, :], in_=b.unsqueeze(0))
+        load_w(1)
+        t0 = 2
+        for n in LOADS[1:]:
+            load_x(t0, n)
             t0 += n
-        state = {"next_load": 0}
 
-        def issue_loads(limit):
-            while state["next_load"] < len(LOADS):
-                li = state["next_load"]
-                n = LOADS[li]
-                first = load_first[li]
-                if first + n > limit:
-                    break
-                x_sb = xpool.tile([P, n, G], BF16, name="x%d" % n, tag="x%d" % n, bufs=XBUFS[n])
-                nc.sync.dma_start(out=x_sb[:], in_=x_view[:, first : first + n, :])
-                x_f = x_sb[:].bitcast(F32)
-                for k in range(n):
-                    x_of[first + k] = (x_f, k)
-                state["next_load"] = li + 1
-
-        issue_loads(LEAD)
+        bias = const.tile([P, J], F32, name="bias")
+        yb = psum.tile([P, J], F32, name="yb", tag="y0")
+        nc.tensor.matmul(out=yb[:], lhsT=ones[:], rhs=brow[:], start=True, stop=True)
+        nc.scalar.copy(
+            out=bias[:].rearrange("q (a e) -> q a e", a=NP),
+            in_=yb[:].rearrange("q (e a) -> q a e", a=NP),
+        )
 
         mk_exp = const.tile([P, 512], BF16, name="mk_exp")
         nc.vector.tensor_copy(
             out=mk_exp[:].rearrange("q (r i) -> q r i", i=8),
             in_=mk[:].unsqueeze(2).to_broadcast([P, 64, 8]),
         )
-        w_grp = const.tile([P, 4096], BF16, name="w_grp", align_bytes=64)
         w_codes = const.tile([P, 1024], U32, name="w_codes", align_bytes=64)
         w_scales = const.tile([P, 1024], U8, name="w_scales", align_bytes=64)
         for g in range(2):
@@ -120,16 +128,6 @@ def tile_featureembed_t_kernel(tc, x, mask, W, b, out):
                 in_=w_grp[:, g * 2048 : (g + 1) * 2048],
             )
 
-        bias = const.tile([P, J], F32, name="bias")
-
-        def make_bias():
-            yb = psum.tile([P, J], F32, name="yb", tag="y0")
-            nc.tensor.matmul(out=yb[:], lhsT=ones[:], rhs=brow[:], start=True, stop=True)
-            nc.scalar.copy(
-                out=bias[:].rearrange("q (a e) -> q a e", a=NP),
-                in_=yb[:].rearrange("q (e a) -> q a e", a=NP),
-            )
-
         run_first = []
         t0 = 0
         for n in RUNS:
@@ -147,18 +145,16 @@ def tile_featureembed_t_kernel(tc, x, mask, W, b, out):
                     chunk_of[run_first[r] + o + k] = (len(chunks), k)
                 chunks.append((run_first[r] + o, w))
             run_chunks.append(mine)
-        store_of = {}
+        store_end = {}
         t0 = 0
-        for si in range(len(STORES)):
-            for k in range(STORES[si]):
-                store_of[t0 + k] = (si, k, t0)
-            t0 += STORES[si]
+        for n in STORES:
+            store_end[t0 + n - 1] = (t0, n)
+            t0 += n
 
         grp_of = {}
         code_of = {}
         o_of = {}
         y_of = {}
-
         xp_of = {}
 
         def permute_tile(t):
@@ -167,14 +163,13 @@ def tile_featureembed_t_kernel(tc, x, mask, W, b, out):
             xp_of[t] = xp
             dst = xp[:].rearrange("p (g u q) -> p g u q", g=2, u=2)
             src = x_f[:, i, :].rearrange("p (g q u) -> p g u q", g=2, u=2)
-            if t % 8 in (1, 3, 6):
+            if vector_permutes(t):
                 nc.vector.tensor_copy(out=dst, in_=src)
             else:
                 nc.scalar.copy(out=dst, in_=src)
 
         def transpose_tile(t):
             q, k = chunk_of[t]
-            w = chunks[q][1]
             if k == 0:
                 grp_of[q] = gpool.tile([P, QW * 1024], BF16, name="grp", tag="grp", align_bytes=64)
             grp_f = grp_of[q][:].bitcast(F32)
@@ -216,28 +211,31 @@ def tile_featureembed_t_kernel(tc, x, mask, W, b, out):
             y_of[t] = y
 
         def add_bias(t):
-            si, k, first = store_of[t]
-            n = STORES[si]
-            if k == 0:
-                o_of[si] = opool.tile([P, n, J], F32, name="o%d" % n, tag="o%d" % n, bufs=OBUFS[n])
-            o_sb = o_of[si]
-            nc.vector.tensor_tensor(out=o_sb[:, k, :], in0=y_of[t][:], in1=bias[:], op=ADD)
-            if k == n - 1:
-                nc.sync.dma_start(out=out_view[:, first : first + n, :], in_=o_sb[:])
+            ci = t // CH
+            if t % CH == 0:
+                si = (18, 19, 16, 17)[ci] if ci < 4 else ci - 4
+                o_of[ci] = slots.tile([P, CH, J], F32, name="o%d" % ci, tag="s%d" % si, align_bytes=64)
+            o_sb = o_of[ci]
+            nc.vector.tensor_tensor(out=o_sb[:, t % CH, :], in0=y_of[t][:], in1=bias[:], op=ADD)
+            if t in store_end:
+                first, n = store_end[t]
+                o = first % CH
+                nc.sync.dma_start(out=out_view[:, first : first + n, :], in_=o_sb[:, o : o + n, :])
 
         NR = len(RUNS)
-        for t in range(RUNS[0]):
-            permute_tile(t)
+
+        def permute_run(r):
+            if r < NR:
+                for t in range(run_first[r], run_first[r] + RUNS[r]):
+                    permute_tile(t)
+
+        for r in range(PL):
+            permute_run(r)
         for s in range(NR + LA):
             if s < NR:
                 for t in range(run_first[s], run_first[s] + RUNS[s]):
                     transpose_tile(t)
-                issue_loads(run_first[s] + RUNS[s] + LEAD)
-            if s + 1 < NR:
-                for t in range(run_first[s + 1], run_first[s + 1] + RUNS[s + 1]):
-                    permute_tile(t)
-            if s == 0:
-                make_bias()
+            permute_run(s + PL)
             m = s - LA
             qs = run_chunks[s] if s < NR else []
             ts = list(range(run_first[m], run_first[m] + RUNS[m])) if m >= 0 else []

@@ -18,7 +18,7 @@ NT = C // P
 FLOPS = 2 * C * G * J
 
 CH = 4
-RUNS = [2, 2] + [4] * 14 + [2, 2]
+RUNS = [2, 2] + [3] * 18 + [2, 2, 2]
 LOADS = [2, 2] + [4] * 15
 STORES = [4] * 15 + [2, 2]
 QW = 2
@@ -26,7 +26,7 @@ GBQ = 6
 CBQ = 6
 XPB = 12
 LA = 1
-PL = 1
+PL = 2
 assert sum(RUNS) == NT and sum(LOADS) == NT and sum(STORES) == NT
 
 

@@ -20,18 +20,19 @@ FLOPS = 2 * C * G * J
 CH = 4
 RUNS = [2, 2] + [3] * 18 + [2, 2, 2]
 LOADS = [2, 2] + [4] * 15
-STORES = [4] * 15 + [2, 2]
+STORES = [4] * 15 + [2, 1, 1]
 QW = 2
 GBQ = 6
 CBQ = 6
 XPB = 12
 LA = 1
+LQ = 0
 PL = 2
 assert sum(RUNS) == NT and sum(LOADS) == NT and sum(STORES) == NT
 
 
-def vector_permutes(t):
-    return t >= 8 and t % 8 in (1, 3, 6)
+def way(t):
+    return "S" if t < 8 else "SVSNSSVS"[t % 8]
 
 
 def tile_featureembed_t_kernel(tc, x, mask, W, b, out):
@@ -158,12 +159,14 @@ def tile_featureembed_t_kernel(tc, x, mask, W, b, out):
         xp_of = {}
 
         def permute_tile(t):
+            if way(t) == "N":
+                return
             x_f, i = x_of[t]
             xp = xppool.tile([P, 512], F32, name="xp", tag="xp")
             xp_of[t] = xp
             dst = xp[:].rearrange("p (g u q) -> p g u q", g=2, u=2)
             src = x_f[:, i, :].rearrange("p (g q u) -> p g u q", g=2, u=2)
-            if vector_permutes(t):
+            if way(t) == "V":
                 nc.vector.tensor_copy(out=dst, in_=src)
             else:
                 nc.scalar.copy(out=dst, in_=src)
@@ -173,10 +176,15 @@ def tile_featureembed_t_kernel(tc, x, mask, W, b, out):
             if k == 0:
                 grp_of[q] = gpool.tile([P, QW * 1024], BF16, name="grp", tag="grp", align_bytes=64)
             grp_f = grp_of[q][:].bitcast(F32)
-            xp = xp_of[t]
             xt = psum.tile([P, 4, P], F32, name="xt%d" % (t % 4), tag="xt%d" % (t % 4))
             for a in range(4):
-                nc.tensor.transpose(xt[:, a, :], xp[:, a * P : (a + 1) * P], ident[:])
+                if way(t) == "N":
+                    x_f, i = x_of[t]
+                    lo = (a // 2) * 256 + a % 2
+                    words = x_f[:, i, lo : (a // 2 + 1) * 256 : 2]
+                else:
+                    words = xp_of[t][:, a * P : (a + 1) * P]
+                nc.tensor.transpose(xt[:, a, :], words, ident[:])
             nc.scalar.copy(
                 out=grp_f[:, k * 512 : (k + 1) * 512].rearrange("q (g c u) -> q g c u", g=2, u=2),
                 in_=xt[:].rearrange("q (g u) c -> q g c u", u=2),
@@ -231,14 +239,14 @@ def tile_featureembed_t_kernel(tc, x, mask, W, b, out):
 
         for r in range(PL):
             permute_run(r)
-        for s in range(NR + LA):
+        for s in range(NR + max(LA, LQ + 1)):
             if s < NR:
                 for t in range(run_first[s], run_first[s] + RUNS[s]):
                     transpose_tile(t)
             permute_run(s + PL)
             m = s - LA
-            qs = run_chunks[s] if s < NR else []
-            ts = list(range(run_first[m], run_first[m] + RUNS[m])) if m >= 0 else []
+            qs = run_chunks[s - LQ] if 0 <= s - LQ < NR else []
+            ts = list(range(run_first[m], run_first[m] + RUNS[m])) if 0 <= m < NR else []
             per = (len(ts) + len(qs) - 1) // len(qs) if qs else len(ts)
             done = 0
             for q in qs:

@@ -24,15 +24,22 @@ STORES = [4] * 15 + [2, 1, 1]
 QW = 2
 GBQ = 6
 CBQ = 6
-XPB = 12
+XPB = 8
+PAIR = True
 LA = 1
 LQ = 0
 PL = 2
+RAMP = 1
+BSTEP = 0
 assert sum(RUNS) == NT and sum(LOADS) == NT and sum(STORES) == NT
 
 
+WAYS = ["SV", "SN", "SS", "VS"]
+EARLY = "NNNNSNSSSNSS"
+
+
 def way(t):
-    return "S" if t < 8 else "SVSNSSVS"[t % 8]
+    return EARLY[t] if t < len(EARLY) else WAYS[t // 2 % len(WAYS)][t % 2]
 
 
 def tile_featureembed_t_kernel(tc, x, mask, W, b, out):
@@ -93,12 +100,14 @@ def tile_featureembed_t_kernel(tc, x, mask, W, b, out):
             t0 += n
 
         bias = const.tile([P, J], F32, name="bias")
-        yb = psum.tile([P, J], F32, name="yb", tag="y0")
-        nc.tensor.matmul(out=yb[:], lhsT=ones[:], rhs=brow[:], start=True, stop=True)
-        nc.scalar.copy(
-            out=bias[:].rearrange("q (a e) -> q a e", a=NP),
-            in_=yb[:].rearrange("q (e a) -> q a e", a=NP),
-        )
+
+        def make_bias():
+            yb = psum.tile([P, J], F32, name="yb", tag="y0")
+            nc.tensor.matmul(out=yb[:], lhsT=ones[:], rhs=brow[:], start=True, stop=True)
+            nc.scalar.copy(
+                out=bias[:].rearrange("q (a e) -> q a e", a=NP),
+                in_=yb[:].rearrange("q (e a) -> q a e", a=NP),
+            )
 
         mk_exp = const.tile([P, 512], BF16, name="mk_exp")
         nc.vector.tensor_copy(
@@ -158,14 +167,15 @@ def tile_featureembed_t_kernel(tc, x, mask, W, b, out):
         y_of = {}
         xp_of = {}
 
-        def permute_tile(t):
+        def permute_tiles(t, n):
             if way(t) == "N":
                 return
             x_f, i = x_of[t]
-            xp = xppool.tile([P, 512], F32, name="xp", tag="xp")
-            xp_of[t] = xp
-            dst = xp[:].rearrange("p (g u q) -> p g u q", g=2, u=2)
-            src = x_f[:, i, :].rearrange("p (g q u) -> p g u q", g=2, u=2)
+            xp = xppool.tile([P, 2, 512], F32, name="xp", tag="xp")
+            for k in range(n):
+                xp_of[t + k] = (xp, k)
+            dst = xp[:, 0:n, :].rearrange("p n (g u q) -> p (n g) u q", g=2, u=2)
+            src = x_f[:, i : i + n, :].rearrange("p n (g q u) -> p (n g) u q", g=2, u=2)
             if way(t) == "V":
                 nc.vector.tensor_copy(out=dst, in_=src)
             else:
@@ -183,7 +193,8 @@ def tile_featureembed_t_kernel(tc, x, mask, W, b, out):
                     lo = (a // 2) * 256 + a % 2
                     words = x_f[:, i, lo : (a // 2 + 1) * 256 : 2]
                 else:
-                    words = xp_of[t][:, a * P : (a + 1) * P]
+                    xp, i = xp_of[t]
+                    words = xp[:, i, a * P : (a + 1) * P]
                 nc.tensor.transpose(xt[:, a, :], words, ident[:])
             nc.scalar.copy(
                 out=grp_f[:, k * 512 : (k + 1) * 512].rearrange("q (g c u) -> q g c u", g=2, u=2),
@@ -221,7 +232,7 @@ def tile_featureembed_t_kernel(tc, x, mask, W, b, out):
         def add_bias(t):
             ci = t // CH
             if t % CH == 0:
-                si = (18, 19, 16, 17)[ci] if ci < 4 else ci - 4
+                si = 16 if ci == 0 else ci - 1
                 o_of[ci] = slots.tile([P, CH, J], F32, name="o%d" % ci, tag="s%d" % si, align_bytes=64)
             o_sb = o_of[ci]
             nc.vector.tensor_tensor(out=o_sb[:, t % CH, :], in0=y_of[t][:], in1=bias[:], op=ADD)
@@ -234,16 +245,28 @@ def tile_featureembed_t_kernel(tc, x, mask, W, b, out):
 
         def permute_run(r):
             if r < NR:
-                for t in range(run_first[r], run_first[r] + RUNS[r]):
-                    permute_tile(t)
+                t = run_first[r]
+                last = run_first[r] + RUNS[r]
+                while t < last:
+                    n = 2 if PAIR and t + 1 < last and way(t) == way(t + 1) and (t + 1) % CH != 0 else 1
+                    permute_tiles(t, n)
+                    t += n
 
-        for r in range(PL):
-            permute_run(r)
+        permuted = [0]
+
+        def permute_upto(n):
+            while permuted[0] < min(n, NR):
+                permute_run(permuted[0])
+                permuted[0] += 1
+
+        permute_upto(1 if RAMP else PL)
         for s in range(NR + max(LA, LQ + 1)):
             if s < NR:
                 for t in range(run_first[s], run_first[s] + RUNS[s]):
                     transpose_tile(t)
-            permute_run(s + PL)
+            if s == BSTEP:
+                make_bias()
+            permute_upto(s + PL + 1 if s >= RAMP else s + 2)
             m = s - LA
             qs = run_chunks[s - LQ] if 0 <= s - LQ < NR else []
             ts = list(range(run_first[m], run_first[m] + RUNS[m])) if 0 <= m < NR else []

@@ -18,24 +18,29 @@ NT = C // P
 FLOPS = 2 * C * G * J
 
 CH = 4
-RUNS = [2, 2] + [3] * 18 + [2, 2, 2]
+RUNS = [2, 2, 2, 2] + [4] * 13 + [2, 2]
 LOADS = [2, 2] + [4] * 15
 STORES = [4] * 15 + [2, 1, 1]
 QW = 2
-GBQ = 6
-CBQ = 6
-XPB = 8
+GBQ = 7
+CBQ = 7
+XPB = 7
 PAIR = True
-LA = 1
-LQ = 0
-PL = 2
-RAMP = 1
+P0 = 4
+PA = 6
+L0 = 4
+L1 = 4
+LS = 4
+QL = 2
+MR = 4
+QFIRST = True
+RAMP = 2
 BSTEP = 0
 assert sum(RUNS) == NT and sum(LOADS) == NT and sum(STORES) == NT
 
 
-WAYS = ["SV", "SN", "SS", "VS"]
-EARLY = "NNNNSNSSSNSS"
+WAYS = ["SS", "VN", "SS", "SV"]
+EARLY = "NNNNNNSSSSSS"
 
 
 def way(t):
@@ -138,23 +143,8 @@ def tile_featureembed_t_kernel(tc, x, mask, W, b, out):
                 in_=w_grp[:, g * 2048 : (g + 1) * 2048],
             )
 
-        run_first = []
-        t0 = 0
-        for n in RUNS:
-            run_first.append(t0)
-            t0 += n
-        chunks = []
-        chunk_of = {}
-        run_chunks = []
-        for r in range(len(RUNS)):
-            mine = []
-            for o in range(0, RUNS[r], QW):
-                w = min(QW, RUNS[r] - o)
-                mine.append(len(chunks))
-                for k in range(w):
-                    chunk_of[run_first[r] + o + k] = (len(chunks), k)
-                chunks.append((run_first[r] + o, w))
-            run_chunks.append(mine)
+        chunks = [(t, QW) for t in range(0, NT, QW)]
+        chunk_of = {t: (t // QW, t % QW) for t in range(NT)}
         store_end = {}
         t0 = 0
         for n in STORES:
@@ -241,43 +231,51 @@ def tile_featureembed_t_kernel(tc, x, mask, W, b, out):
                 o = first % CH
                 nc.sync.dma_start(out=out_view[:, first : first + n, :], in_=o_sb[:, o : o + n, :])
 
-        NR = len(RUNS)
-
-        def permute_run(r):
-            if r < NR:
-                t = run_first[r]
-                last = run_first[r] + RUNS[r]
-                while t < last:
-                    n = 2 if PAIR and t + 1 < last and way(t) == way(t + 1) and (t + 1) % CH != 0 else 1
-                    permute_tiles(t, n)
-                    t += n
-
         permuted = [0]
+        quantised = [0]
+        multiplied = [0]
 
         def permute_upto(n):
-            while permuted[0] < min(n, NR):
-                permute_run(permuted[0])
-                permuted[0] += 1
+            t = permuted[0]
+            while t < min(n, NT):
+                k = 2 if PAIR and t + 1 < min(n, NT) and way(t) == way(t + 1) and (t + 1) % CH != 0 else 1
+                permute_tiles(t, k)
+                t += k
+            permuted[0] = max(t, permuted[0])
 
-        permute_upto(1 if RAMP else PL)
-        for s in range(NR + max(LA, LQ + 1)):
-            if s < NR:
-                for t in range(run_first[s], run_first[s] + RUNS[s]):
-                    transpose_tile(t)
+        steps = len(RUNS)
+        permute_upto(P0)
+        done = 0
+        s = 0
+        while multiplied[0] < NT:
+            n = RUNS[s] if s < steps else 0
+            for t in range(done, done + n):
+                transpose_tile(t)
+            done += n
             if s == BSTEP:
                 make_bias()
-            permute_upto(s + PL + 1 if s >= RAMP else s + 2)
-            m = s - LA
-            qs = run_chunks[s - LQ] if 0 <= s - LQ < NR else []
-            ts = list(range(run_first[m], run_first[m] + RUNS[m])) if 0 <= m < NR else []
-            per = (len(ts) + len(qs) - 1) // len(qs) if qs else len(ts)
-            done = 0
-            for q in qs:
-                quantise(q)
-                for t in ts[done : done + per]:
+            permute_upto(done + (PA if s >= RAMP else P0))
+            lag = max(L1, L0 - s // LS) if done < NT else 0
+            want_q = (NT if done == NT else done - QL) // QW
+            qs = list(range(quantised[0], max(quantised[0], want_q)))
+            quantised[0] = max(quantised[0], want_q)
+            limit = quantised[0] * QW
+            if done < NT:
+                want_m = min(done - lag, limit)
+            else:
+                want_m = min(multiplied[0] + MR, limit)
+            ts = list(range(multiplied[0], max(multiplied[0], want_m)))
+            multiplied[0] = max(multiplied[0], want_m)
+            for j in range(max(len(qs), 1)):
+                for q in qs[j : j + 1]:
+                    if QFIRST:
+                        quantise(q)
+                a = len(ts) * j // max(len(qs), 1)
+                e = len(ts) * (j + 1) // max(len(qs), 1)
+                for t in ts[a:e]:
                     multiply(t)
                     add_bias(t)
-                done += per
-            for t in ts[done:]:
-                multiply(t)
-                add_bias(t)
+                for q in qs[j : j + 1]:
+                    if not QFIRST:
+                        quantise(q)
+            s += 1

@@ -49,8 +49,10 @@ def way(t):
 
 def tile_featureembed_t_kernel(tc, x, mask, W, b, out):
     nc = tc.nc
-    x_view = x.rearrange("(p t) k -> p t k", t=NT)
-    out_view = out.rearrange("(p t) a e -> p t (a e)", t=NT)
+    x_view = [x[c * CH * P : (c + 1) * CH * P, :].rearrange("(p i) k -> p i k", i=CH) for c in range(NT // CH)]
+    out_view = [
+        out[c * CH * P : (c + 1) * CH * P, :, :].rearrange("(p i) a e -> p i (a e)", i=CH) for c in range(NT // CH)
+    ]
 
     with ExitStack() as ctx:
         const = ctx.enter_context(tc.tile_pool(name="const", bufs=1))
@@ -91,7 +93,7 @@ def tile_featureembed_t_kernel(tc, x, mask, W, b, out):
                 x_slots[ci] = slots.tile([P, CH, G], BF16, name="x%d" % ci, tag="s%d" % ci, align_bytes=64)
             x_sb = x_slots[ci]
             o = first % CH
-            nc.sync.dma_start(out=x_sb[:, o : o + n, :], in_=x_view[:, first : first + n, :])
+            nc.sync.dma_start(out=x_sb[:, o : o + n, :], in_=x_view[ci][:, o : o + n, :])
             for k in range(n):
                 x_of[first + k] = (x_sb[:].bitcast(F32), o + k)
 
@@ -229,7 +231,7 @@ def tile_featureembed_t_kernel(tc, x, mask, W, b, out):
             if t in store_end:
                 first, n = store_end[t]
                 o = first % CH
-                nc.sync.dma_start(out=out_view[:, first : first + n, :], in_=o_sb[:, o : o + n, :])
+                nc.sync.dma_start(out=out_view[ci][:, o : o + n, :], in_=o_sb[:, o : o + n, :])
 
         permuted = [0]
         quantised = [0]

from contextlib import ExitStack

import concourse.mybir as mybir
from concourse.masks import make_identity

F32 = mybir.dt.float32
BF16 = mybir.dt.bfloat16
U32 = mybir.dt.uint32
U8 = mybir.dt.uint8
FP8X4 = mybir.dt.float8_e4m3fn_x4
ADD = mybir.AluOpType.add
MULT = mybir.AluOpType.mult

C, G, NP, E = 8192, 1024, 8, 64
J = NP * E
P = 128
NT = C // P
FLOPS = 2 * C * G * J

CH = 4
RUNS = [2, 2, 2, 2] + [4] * 13 + [2, 2]
LOADS = [2, 2] + [4] * 15
STORES = [4] * 15 + [2, 1, 1]
QW = 2
GBQ = 7
CBQ = 7
XPB = 7
PAIR = True
P0 = 4
PA = 6
L0 = 4
L1 = 4
LS = 4
QL = 2
MR = 4
QFIRST = True
RAMP = 2
BSTEP = 0
assert sum(RUNS) == NT and sum(LOADS) == NT and sum(STORES) == NT


WAYS = ["SS", "VN", "SS", "SV"]
EARLY = "NNNNNNSSSSSS"


def way(t):
    return EARLY[t] if t < len(EARLY) else WAYS[t // 2 % len(WAYS)][t % 2]


def tile_featureembed_t_kernel(tc, x, mask, W, b, out):
    nc = tc.nc
    x_view = [x[c * CH * P : (c + 1) * CH * P, :].rearrange("(p i) k -> p i k", i=CH) for c in range(NT // CH)]
    out_view = [
        out[c * CH * P : (c + 1) * CH * P, :, :].rearrange("(p i) a e -> p i (a e)", i=CH) for c in range(NT // CH)
    ]

    with ExitStack() as ctx:
        const = ctx.enter_context(tc.tile_pool(name="const", bufs=1))
        slots = ctx.enter_context(tc.tile_pool(name="slots", bufs=1))
        xppool = ctx.enter_context(tc.tile_pool(name="xppool", bufs=XPB))
        gpool = ctx.enter_context(tc.tile_pool(name="gpool", bufs=GBQ))
        cpool = ctx.enter_context(tc.tile_pool(name="cpool", bufs=CBQ))
        psum = ctx.enter_context(tc.psum_pool(name="psum", bufs=1))
        ctx.enter_context(tc.manual_schedule())

        brow = const.tile([P, J], BF16, name="brow")
        ones = const.tile([P, P], BF16, name="ones")
        ident = const.tile([P, P], F32, name="ident")
        nc.gpsimd.memset(brow[:], 0.0)
        nc.gpsimd.memset(ones[:], 1.0)
        make_identity(nc, ident[:])

        mk = const.tile([P, 64], BF16, name="mk")
        nc.sync.dma_start(
            out=mk[:].rearrange("q (g r) -> q g r", g=2),
            in_=mask.rearrange("(g q t) m -> q g (t m)", g=2, q=P, t=4),
        )
        w_raw = slots.tile([P, 4096], BF16, name="w_raw", tag="s16", align_bytes=64)
        w_grp = slots.tile([P, 4096], BF16, name="w_grp", tag="s17", align_bytes=64)

        def load_w(g):
            nc.sync.dma_start(
                out=w_raw[:, g * 2048 : (g + 1) * 2048],
                in_=W[g * 512 : (g + 1) * 512, :].rearrange("(q t) j -> q (t j)", t=4),
            )

        x_of = {}
        x_slots = {}

        def load_x(first, n):
            ci = first // CH
            if ci not in x_slots:
                x_slots[ci] = slots.tile([P, CH, G], BF16, name="x%d" % ci, tag="s%d" % ci, align_bytes=64)
            x_sb = x_slots[ci]
            o = first % CH
            nc.sync.dma_start(out=x_sb[:, o : o + n, :], in_=x_view[ci][:, o : o + n, :])
            for k in range(n):
                x_of[first + k] = (x_sb[:].bitcast(F32), o + k)

        load_w(0)
        load_x(0, 2)
        nc.sync.dma_start(out=brow[0:1, :], in_=b.unsqueeze(0))
        load_w(1)
        t0 = 2
        for n in LOADS[1:]:
            load_x(t0, n)
            t0 += n

        bias = const.tile([P, J], F32, name="bias")

        def make_bias():
            yb = psum.tile([P, J], F32, name="yb", tag="y0")
            nc.tensor.matmul(out=yb[:], lhsT=ones[:], rhs=brow[:], start=True, stop=True)
            nc.scalar.copy(
                out=bias[:].rearrange("q (a e) -> q a e", a=NP),
                in_=yb[:].rearrange("q (e a) -> q a e", a=NP),
            )

        mk_exp = const.tile([P, 512], BF16, name="mk_exp")
        nc.vector.tensor_copy(
            out=mk_exp[:].rearrange("q (r i) -> q r i", i=8),
            in_=mk[:].unsqueeze(2).to_broadcast([P, 64, 8]),
        )
        w_codes = const.tile([P, 1024], U32, name="w_codes", align_bytes=64)
        w_scales = const.tile([P, 1024], U8, name="w_scales", align_bytes=64)
        for g in range(2):
            for h in range(2):
                nc.vector.tensor_tensor(
                    out=w_grp[:, g * 2048 + h * 1024 : g * 2048 + (h + 1) * 1024].rearrange(
                        "q (a e t) -> q e t a", a=4, t=4
                    ),
                    in0=w_raw[:, g * 2048 : (g + 1) * 2048].rearrange("q (t e a) -> q e t a", t=4, a=NP)[
                        :, :, :, h * 4 : (h + 1) * 4
                    ],
                    in1=mk_exp[:, g * 256 : (g + 1) * 256]
                    .rearrange("q (t e) -> q e t", t=4)
                    .unsqueeze(3)
                    .to_broadcast([P, E, 4, 4]),
                    op=MULT,
                )
        for g in range(2):
            nc.vector.quantize_mx(
                out=w_codes[:, g * 512 : (g + 1) * 512].bitcast(FP8X4),
                scales=w_scales[:, g * 512 : (g + 1) * 512],
                in_=w_grp[:, g * 2048 : (g + 1) * 2048],
            )

        chunks = [(t, QW) for t in range(0, NT, QW)]
        chunk_of = {t: (t // QW, t % QW) for t in range(NT)}
        store_end = {}
        t0 = 0
        for n in STORES:
            store_end[t0 + n - 1] = (t0, n)
            t0 += n

        grp_of = {}
        code_of = {}
        o_of = {}
        y_of = {}
        xp_of = {}

        def permute_tiles(t, n):
            if way(t) == "N":
                return
            x_f, i = x_of[t]
            xp = xppool.tile([P, 2, 512], F32, name="xp", tag="xp")
            for k in range(n):
                xp_of[t + k] = (xp, k)
            dst = xp[:, 0:n, :].rearrange("p n (g u q) -> p (n g) u q", g=2, u=2)
            src = x_f[:, i : i + n, :].rearrange("p n (g q u) -> p (n g) u q", g=2, u=2)
            if way(t) == "V":
                nc.vector.tensor_copy(out=dst, in_=src)
            else:
                nc.scalar.copy(out=dst, in_=src)

        def transpose_tile(t):
            q, k = chunk_of[t]
            if k == 0:
                grp_of[q] = gpool.tile([P, QW * 1024], BF16, name="grp", tag="grp", align_bytes=64)
            grp_f = grp_of[q][:].bitcast(F32)
            xt = psum.tile([P, 4, P], F32, name="xt%d" % (t % 4), tag="xt%d" % (t % 4))
            for a in range(4):
                if way(t) == "N":
                    x_f, i = x_of[t]
                    lo = (a // 2) * 256 + a % 2
                    words = x_f[:, i, lo : (a // 2 + 1) * 256 : 2]
                else:
                    xp, i = xp_of[t]
                    words = xp[:, i, a * P : (a + 1) * P]
                nc.tensor.transpose(xt[:, a, :], words, ident[:])
            nc.scalar.copy(
                out=grp_f[:, k * 512 : (k + 1) * 512].rearrange("q (g c u) -> q g c u", g=2, u=2),
                in_=xt[:].rearrange("q (g u) c -> q g c u", u=2),
            )

        def quantise(q):
            w = chunks[q][1]
            codes = cpool.tile([P, QW * 256], U32, name="codes", tag="codes", align_bytes=64)
            scales = cpool.tile([P, QW * 256], U8, name="scales", tag="scales", align_bytes=64)
            code_of[q] = (codes, scales)
            nc.vector.quantize_mx(
                out=codes[:, 0 : w * 256].bitcast(FP8X4),
                scales=scales[:, 0 : w * 256],
                in_=grp_of[q][:, 0 : w * 1024],
            )

        def multiply(t):
            q, k = chunk_of[t]
            codes, scales = code_of[q]
            y = psum.tile([P, J], F32, name="y%d" % (t % 4), tag="y%d" % (t % 4))
            for g in range(2):
                cols = slice((k * 2 + g) * P, (k * 2 + g + 1) * P)
                nc.tensor.matmul_mx(
                    out=y[:],
                    lhsT=codes[:, cols].bitcast(FP8X4),
                    lhsT_scale=scales[:, cols],
                    rhs=w_codes[:, g * 512 : (g + 1) * 512].bitcast(FP8X4),
                    rhs_scale=w_scales[:, g * 512 : (g + 1) * 512],
                    start=(g == 0),
                    stop=(g == 1),
                )
            y_of[t] = y

        def add_bias(t):
            ci = t // CH
            if t % CH == 0:
                si = 16 if ci == 0 else ci - 1
                o_of[ci] = slots.tile([P, CH, J], F32, name="o%d" % ci, tag="s%d" % si, align_bytes=64)
            o_sb = o_of[ci]
            nc.vector.tensor_tensor(out=o_sb[:, t % CH, :], in0=y_of[t][:], in1=bias[:], op=ADD)
            if t in store_end:
                first, n = store_end[t]
                o = first % CH
                nc.sync.dma_start(out=out_view[ci][:, o : o + n, :], in_=o_sb[:, o : o + n, :])

        permuted = [0]
        quantised = [0]
        multiplied = [0]

        def permute_upto(n):
            t = permuted[0]
            while t < min(n, NT):
                k = 2 if PAIR and t + 1 < min(n, NT) and way(t) == way(t + 1) and (t + 1) % CH != 0 else 1
                permute_tiles(t, k)
                t += k
            permuted[0] = max(t, permuted[0])

        steps = len(RUNS)
        permute_upto(P0)
        done = 0
        s = 0
        while multiplied[0] < NT:
            n = RUNS[s] if s < steps else 0
            for t in range(done, done + n):
                transpose_tile(t)
            done += n
            if s == BSTEP:
                make_bias()
            permute_upto(done + (PA if s >= RAMP else P0))
            lag = max(L1, L0 - s // LS) if done < NT else 0
            want_q = (NT if done == NT else done - QL) // QW
            qs = list(range(quantised[0], max(quantised[0], want_q)))
            quantised[0] = max(quantised[0], want_q)
            limit = quantised[0] * QW
            if done < NT:
                want_m = min(done - lag, limit)
            else:
                want_m = min(multiplied[0] + MR, limit)
            ts = list(range(multiplied[0], max(multiplied[0], want_m)))
            multiplied[0] = max(multiplied[0], want_m)
            for j in range(max(len(qs), 1)):
                for q in qs[j : j + 1]:
                    if QFIRST:
                        quantise(q)
                a = len(ts) * j // max(len(qs), 1)
                e = len(ts) * (j + 1) // max(len(qs), 1)
                for t in ts[a:e]:
                    multiply(t)
                    add_bias(t)
                for q in qs[j : j + 1]:
                    if not QFIRST:
                        quantise(q)
            s += 1
